import numpy as np
import ml_dtypes


def mxq(x, axis, fmt="e4m3"):
    dtype, down = {"e4m3": (ml_dtypes.float8_e4m3fn, 7), "e5m2": (ml_dtypes.float8_e5m2, 14)}[fmt]
    v = np.moveaxis(np.asarray(x, np.float32).astype(ml_dtypes.bfloat16).astype(np.float64), axis, -1)
    blocks = v.reshape(v.shape[:-1] + (-1, 32))
    amax = np.abs(blocks).max(-1, keepdims=True)
    byte = np.maximum(np.where(amax > 0, np.frexp(amax)[1] - 1 + 127, 0) - down, 1)
    scale = np.exp2(byte - 127.0)
    codes = (blocks / scale).astype(np.float32).astype(dtype).astype(np.float64)
    return np.moveaxis((codes * scale).reshape(v.shape), -1, axis)


WIDE = False


def mx_kscale(k):
    if not WIDE:
        return np.ones(k)
    levels = np.array([10, -10, 5, -5, 0])
    a = np.random.permutation(np.resize(levels, k // 512 * 4)).reshape(k // 512, 4)
    idx = np.arange(k)
    return np.exp2(a[idx // 512, idx % 128 // 32])


BF16 = ml_dtypes.bfloat16


def bf(x):
    return np.asarray(x, np.float32).astype(BF16)


def f64(x):
    return np.asarray(x).astype(np.float64)


B, N_IN, N_OUT, D_IN, D_OUT = 128, 64, 16, 512, 16


def setup_inputs():
    s = mx_kscale(D_IN)
    inputs = np.random.standard_normal((B, N_IN, D_IN, 1)) * s[:, None]
    transform_mat = np.random.uniform(-1.0, 1.0, (1, N_IN, N_OUT, D_IN, D_OUT, 1)) * np.sqrt(3.0 / D_IN) / s[:, None, None]
    return {"inputs": bf(inputs), "transform_mat": bf(transform_mat)}


def reference(inputs, transform_mat):
    xq = mxq(f64(inputs)[..., 0], 2, "e4m3")
    wq = mxq(f64(transform_mat)[0, ..., 0], 2, "e4m3")
    prod = xq.transpose(1, 0, 2) @ wq.transpose(0, 2, 1, 3).reshape(N_IN, D_IN, N_OUT * D_OUT)
    votes = prod.reshape(N_IN, B, N_OUT, D_OUT).transpose(1, 0, 2, 3)
    return votes[..., None]

@@ -1,0 +1,175 @@
+from contextlib import ExitStack
+
+import concourse.mybir as mybir
+from concourse.masks import make_identity
+
+F32 = mybir.dt.float32
+BF16 = mybir.dt.bfloat16
+U32 = mybir.dt.uint32
+U8 = mybir.dt.uint8
+FP8X4 = mybir.dt.float8_e4m3fn_x4
+
+P = 128
+N_IN = 64
+N_OUT = 16
+D_IN = 512
+D_OUT = 16
+COLS = N_OUT * D_OUT
+CH = 8
+N_CH = N_IN // CH
+GR = 4
+N_GR = N_IN // GR
+PAIRS = D_OUT // 2
+N_BANKS = N_CH * PAIRS
+W_BUFS = 5
+X_BUFS = 5
+VEC_BANKS = (1, 3, 5, 20, 36, 52)
+
+FLOPS = 2 * P * N_IN * D_IN * COLS
+
+
+def tile_transforming_kernel(tc, inputs, transform_mat, out):
+    nc = tc.nc
+    w_view = transform_mat.rearrange("z (c n) m i o x -> c (z n m) (i o x)", c=N_CH)
+    x_view = inputs.rearrange("b (c n) i x -> c b (n i x)", c=N_CH)
+    o_view = out.rearrange("b (g n) m o x -> g b (n m o x)", g=N_GR)
+    oc_view = out.rearrange("b (c n) m o x -> c b (n m o x)", c=N_CH)
+
+    with ExitStack() as stack:
+        const = stack.enter_context(tc.tile_pool(name="const", bufs=1))
+        w_pool = stack.enter_context(tc.tile_pool(name="w_pool", bufs=W_BUFS))
+        x_pool = stack.enter_context(tc.tile_pool(name="x_pool", bufs=X_BUFS))
+        g_pool = stack.enter_context(tc.tile_pool(name="g_pool", bufs=2))
+        xg_pool = stack.enter_context(tc.tile_pool(name="xg_pool", bufs=2))
+        wq_pool = stack.enter_context(tc.tile_pool(name="wq_pool", bufs=3))
+        xq_pool = stack.enter_context(tc.tile_pool(name="xq_pool", bufs=5))
+        o_pool = stack.enter_context(tc.tile_pool(name="o_pool", bufs=3))
+        psum_w = stack.enter_context(tc.psum_pool(name="psum_w", bufs=4))
+        psum_x = stack.enter_context(tc.psum_pool(name="psum_x", bufs=2))
+        psum_o = stack.enter_context(tc.psum_pool(name="psum_o", bufs=2))
+
+        ident = const.tile([P, P], F32)
+        make_identity(nc, ident[:])
+
+        w_raw = {}
+        x_raw = {}
+        w_grp = {}
+        w_codes = {}
+        w_scales = {}
+        x_codes = {}
+        x_scales = {}
+        x_grp = {}
+        o_sb = {}
+
+        def load_w(c):
+            t = w_pool.tile([P, D_IN * D_OUT], BF16, name="w_raw")
+            nc.sync.dma_start(out=t[:], in_=w_view[c])
+            w_raw[c] = t
+
+        def load_x(c):
+            t = x_pool.tile([P, CH * D_IN], BF16, name="x_raw")
+            nc.sync.dma_start(out=t[:], in_=x_view[c])
+            x_raw[c] = t
+
+        def w_bank(g):
+            c, j = divmod(g, PAIRS)
+            if j == 0:
+                w_grp[c] = g_pool.tile([P, CH, PAIRS, 2 * N_OUT, 4], BF16, name="w_grp", align_bytes=64)
+            words = w_raw[c][:].bitcast(F32).rearrange("r (u a e j) -> r u e j a", u=2, a=P, e=2, j=PAIRS)
+            wt = psum_w.tile([P, 512], F32, name="wt")
+            for u in range(2):
+                for e in range(2):
+                    t = 2 * u + e
+                    nc.tensor.transpose(wt[:, t * P : (t + 1) * P], words[:, u, e, j, :], ident[:])
+            src = wt[:].bitcast(BF16).rearrange("p (t n c) -> p n c t", t=4, n=CH)
+            if g in VEC_BANKS:
+                nc.vector.tensor_copy(out=w_grp[c][:, :, j, :, :], in_=src)
+            else:
+                nc.scalar.copy(out=w_grp[c][:, :, j, :, :], in_=src)
+
+        def x_group(q):
+            c, half = divmod(q, 2)
+            words = x_raw[c][:].bitcast(F32).rearrange("b (n u a) -> b n u a", n=CH, u=2)
+            x_grp[q] = xg_pool.tile([P, GR * D_IN], BF16, name="x_grp", align_bytes=64)
+            dst = x_grp[q][:].bitcast(F32).rearrange("p (h n b u) -> p h n b u", h=2, n=2, u=2)
+            for h in range(2):
+                xt = psum_x.tile([P, 2, 2, P], F32, name="xt")
+                for n in range(2):
+                    for u in range(2):
+                        nc.tensor.transpose(xt[:, n, u, :], words[:, GR * half + 2 * h + n, u, :], ident[:])
+                nc.vector.tensor_copy(out=dst[:, h], in_=xt[:].rearrange("p n u b -> p n b u"))
+
+        def x_quant(q):
+            x_codes[q] = xq_pool.tile([P, GR * P], U32, name="x_codes", align_bytes=64)
+            x_scales[q] = xq_pool.tile([P, GR * P], U8, name="x_scales", align_bytes=64)
+            nc.vector.quantize_mx(out=x_codes[q][:].bitcast(FP8X4), scales=x_scales[q][:], in_=x_grp[q][:])
+
+        def w_quant(q):
+            c, half = divmod(q, 2)
+            w_codes[q] = wq_pool.tile([P, GR * COLS], U32, name="w_codes", align_bytes=64)
+            w_scales[q] = wq_pool.tile([P, GR * COLS], U8, name="w_scales", align_bytes=64)
+            nc.vector.quantize_mx(
+                out=w_codes[q][:].bitcast(FP8X4),
+                scales=w_scales[q][:],
+                in_=w_grp[c][:, GR * half : GR * (half + 1)].rearrange("p n j c t -> p (n j c t)"),
+            )
+
+        def multiply(q):
+            c, half = divmod(q, 2)
+            last = c == N_CH - 1
+            if half == 0:
+                o_sb[c] = o_pool.tile([P, CH, COLS], F32, name="o_sb")
+            for h in range(2):
+                acc = psum_o.tile([P, 2, COLS], F32, name="acc")
+                for n in range(2):
+                    a = 2 * h + n
+                    nc.tensor.matmul_mx(
+                        out=acc[:, n, :],
+                        lhsT=x_codes[q][:, a * P : (a + 1) * P].bitcast(FP8X4),
+                        lhsT_scale=x_scales[q][:, a * P : (a + 1) * P],
+                        rhs=w_codes[q][:, a * COLS : (a + 1) * COLS].bitcast(FP8X4),
+                        rhs_scale=w_scales[q][:, a * COLS : (a + 1) * COLS],
+                        start=True,
+                        stop=True,
+                    )
+                n0 = GR * half + 2 * h
+                if last and h == 1:
+                    for n in range(2):
+                        nc.scalar.copy(
+                            out=o_sb[c][:, n0 + n, :].rearrange("p (m j e) -> p m j e", m=N_OUT, j=PAIRS),
+                            in_=acc[:, n, :].rearrange("p (j m e) -> p m j e", j=PAIRS, m=N_OUT),
+                        )
+                else:
+                    nc.vector.tensor_copy(
+                        out=o_sb[c][:, n0 : n0 + 2, :].rearrange("p n (m j e) -> p n m j e", m=N_OUT, j=PAIRS),
+                        in_=acc[:].rearrange("p n (j m e) -> p n m j e", j=PAIRS, m=N_OUT),
+                    )
+            if last:
+                nc.sync.dma_start(
+                    out=o_view[q], in_=o_sb[c][:, GR * half : GR * (half + 1), :].rearrange("p n c -> p (n c)")
+                )
+            elif half == 1:
+                nc.sync.dma_start(out=oc_view[c], in_=o_sb[c][:].rearrange("p n c -> p (n c)"))
+
+        with tc.manual_schedule():
+            for c in range(W_BUFS):
+                load_w(c)
+                load_x(c)
+            for g in range(4):
+                w_bank(g)
+            for s in range(N_GR + 3):
+                if s < N_GR:
+                    x_group(s)
+                    if s % 2 == 1 and s // 2 + X_BUFS < N_CH:
+                        load_x(s // 2 + X_BUFS)
+                if 0 <= s - 2 < N_GR:
+                    w_quant(s - 2)
+                if s < N_GR:
+                    x_quant(s)
+                if 0 <= s - 3 < N_GR:
+                    multiply(s - 3)
+                if s < N_GR - 1:
+                    for g in range(4 * s + 4, 4 * s + 8):
+                        w_bank(g)
+                    if s % 2 == 0 and s // 2 + W_BUFS < N_CH:
+                        load_w(s // 2 + W_BUFS)

@@ -8,6 +8,8 @@ BF16 = mybir.dt.bfloat16
 U32 = mybir.dt.uint32
 U8 = mybir.dt.uint8
 FP8X4 = mybir.dt.float8_e4m3fn_x4
+MULT = mybir.AluOpType.mult
+ADD = mybir.AluOpType.add
 
 P = 128
 N_IN = 64
@@ -15,161 +17,234 @@ N_OUT = 16
 D_IN = 512
 D_OUT = 16
 COLS = N_OUT * D_OUT
-CH = 8
-N_CH = N_IN // CH
 GR = 4
-N_GR = N_IN // GR
-PAIRS = D_OUT // 2
-N_BANKS = N_CH * PAIRS
-W_BUFS = 5
+N_Q = N_IN // GR
+W_BUFS = 8
 X_BUFS = 5
-VEC_BANKS = (1, 3, 5, 20, 36, 52)
+ROUTE = ["vsss","gsss","gsss","gsss","gsss","gsss","gsss","gsss","gsss","gsss","gsss","gsss","gsss","gsss","gsss","vsss"]
+EVAC = ["vs","vs","vs","vs","vs","vs","vs","vs","vs","vs","vs","vs","vs","ss","vs","vs"]
 
 FLOPS = 2 * P * N_IN * D_IN * COLS
 
 
 def tile_transforming_kernel(tc, inputs, transform_mat, out):
     nc = tc.nc
-    w_view = transform_mat.rearrange("z (c n) m i o x -> c (z n m) (i o x)", c=N_CH)
-    x_view = inputs.rearrange("b (c n) i x -> c b (n i x)", c=N_CH)
-    o_view = out.rearrange("b (g n) m o x -> g b (n m o x)", g=N_GR)
-    oc_view = out.rearrange("b (c n) m o x -> c b (n m o x)", c=N_CH)
+    w_view = transform_mat.rearrange("z (q n) m (u i) o x -> q (z n m u) (i o x)", q=N_Q, u=2)
+    x_view = inputs.rearrange("b n i x -> b (n i x)")
+    o_view = out.rearrange("b n m o x -> b (n m o x)")
 
     with ExitStack() as stack:
         const = stack.enter_context(tc.tile_pool(name="const", bufs=1))
         w_pool = stack.enter_context(tc.tile_pool(name="w_pool", bufs=W_BUFS))
         x_pool = stack.enter_context(tc.tile_pool(name="x_pool", bufs=X_BUFS))
-        g_pool = stack.enter_context(tc.tile_pool(name="g_pool", bufs=2))
+        g_pool = stack.enter_context(tc.tile_pool(name="g_pool", bufs=3))
+        t_pool = stack.enter_context(tc.tile_pool(name="t_pool", bufs=2))
         xg_pool = stack.enter_context(tc.tile_pool(name="xg_pool", bufs=2))
         wq_pool = stack.enter_context(tc.tile_pool(name="wq_pool", bufs=3))
-        xq_pool = stack.enter_context(tc.tile_pool(name="xq_pool", bufs=5))
-        o_pool = stack.enter_context(tc.tile_pool(name="o_pool", bufs=3))
+        xq_pool = stack.enter_context(tc.tile_pool(name="xq_pool", bufs=4))
+        o_pool = stack.enter_context(tc.tile_pool(name="o_pool", bufs=5))
         psum_w = stack.enter_context(tc.psum_pool(name="psum_w", bufs=4))
         psum_x = stack.enter_context(tc.psum_pool(name="psum_x", bufs=2))
         psum_o = stack.enter_context(tc.psum_pool(name="psum_o", bufs=2))
 
         ident = const.tile([P, P], F32)
         make_identity(nc, ident[:])
+        perm = const.tile([P, P], F32)
+        nc.vector.tensor_copy(
+            out=perm[:].rearrange("k (u g) -> k u g", u=2), in_=ident[:].rearrange("k (g u) -> k u g", u=2)
+        )
 
         w_raw = {}
         x_raw = {}
+        w_bank = {}
+        x_bank = {}
         w_grp = {}
         w_codes = {}
         w_scales = {}
         x_codes = {}
         x_scales = {}
         x_grp = {}
+        acc = {}
         o_sb = {}
 
-        def load_w(c):
-            t = w_pool.tile([P, D_IN * D_OUT], BF16, name="w_raw")
-            nc.sync.dma_start(out=t[:], in_=w_view[c])
-            w_raw[c] = t
+        def load_w(q):
+            w_raw[q] = w_pool.tile([P, D_IN * D_OUT // 2], BF16, name="w_raw")
+            nc.sync.dma_start(out=w_raw[q][:], in_=w_view[q])
 
-        def load_x(c):
-            t = x_pool.tile([P, CH * D_IN], BF16, name="x_raw")
-            nc.sync.dma_start(out=t[:], in_=x_view[c])
-            x_raw[c] = t
+        def load_x(q0, nq):
+            t = x_pool.tile([P, 2 * GR * D_IN], BF16, name="x_raw")
+            width = nq * GR * D_IN
+            nc.sync.dma_start(out=t[:, 0:width], in_=x_view[:, q0 * GR * D_IN : q0 * GR * D_IN + width])
+            for k in range(nq):
+                x_raw[q0 + k] = t[:, k * GR * D_IN : (k + 1) * GR * D_IN]
 
-        def w_bank(g):
-            c, j = divmod(g, PAIRS)
-            if j == 0:
-                w_grp[c] = g_pool.tile([P, CH, PAIRS, 2 * N_OUT, 4], BF16, name="w_grp", align_bytes=64)
-            words = w_raw[c][:].bitcast(F32).rearrange("r (u a e j) -> r u e j a", u=2, a=P, e=2, j=PAIRS)
-            wt = psum_w.tile([P, 512], F32, name="wt")
-            for u in range(2):
-                for e in range(2):
-                    t = 2 * u + e
-                    nc.tensor.transpose(wt[:, t * P : (t + 1) * P], words[:, u, e, j, :], ident[:])
-            src = wt[:].bitcast(BF16).rearrange("p (t n c) -> p n c t", t=4, n=CH)
-            if g in VEC_BANKS:
-                nc.vector.tensor_copy(out=w_grp[c][:, :, j, :, :], in_=src)
+        def w_transposes(q):
+            words = w_raw[q][:].bitcast(F32).rearrange("r (a e j) -> r e j a", e=2, j=8)
+            for g in range(4):
+                wt = psum_w.tile([P, 512], F32, name="wt")
+                w_bank[(q, g)] = wt
+                dst = wt[:].rearrange("p (u e n k m) -> p e k u n m", u=2, e=2, n=GR, k=2)
+                for k in range(2):
+                    for e in range(2):
+                        nc.tensor.transpose(dst[:, e, k], words[:, e, 2 * g + k, :], perm[:])
+
+        def w_copy(q, g):
+            if q not in w_grp:
+                w_grp[q] = g_pool.tile([P, GR, 4, 64, 4], BF16, name="w_grp", align_bytes=64)
+            wt = w_bank[(q, g)]
+            dst = w_grp[q][:, :, g, :, :]
+            route = ROUTE[q][g]
+            if route == "g":
+                tmp = t_pool.tile([P, 512], F32, name="tmp")
+                nc.vector.tensor_copy(out=tmp[:], in_=wt[:])
+                nc.gpsimd.tensor_scalar(
+                    out=dst,
+                    in0=tmp[:].bitcast(BF16).rearrange("p (t n c) -> p n c t", t=4, n=GR),
+                    scalar1=1.0,
+                    scalar2=0.0,
+                    op0=MULT,
+                    op1=ADD,
+                )
             else:
-                nc.scalar.copy(out=w_grp[c][:, :, j, :, :], in_=src)
+                src = wt[:].bitcast(BF16).rearrange("p (t n c) -> p n c t", t=4, n=GR)
+                if route == "v":
+                    nc.vector.tensor_copy(out=dst, in_=src)
+                else:
+                    nc.scalar.copy(out=dst, in_=src)
 
-        def x_group(q):
-            c, half = divmod(q, 2)
-            words = x_raw[c][:].bitcast(F32).rearrange("b (n u a) -> b n u a", n=CH, u=2)
+        def x_transposes(q):
+            words = x_raw[q].bitcast(F32).rearrange("b (n u a) -> b n u a", n=GR, u=2)
+            for h in range(2):
+                xt = psum_x.tile([P, 2, 2, P], F32, name="xt")
+                x_bank[(q, h)] = xt
+                for n in range(2):
+                    for u in range(2):
+                        nc.tensor.transpose(xt[:, n, u, :], words[:, 2 * h + n, u, :], ident[:])
+
+        def x_copy(q):
             x_grp[q] = xg_pool.tile([P, GR * D_IN], BF16, name="x_grp", align_bytes=64)
             dst = x_grp[q][:].bitcast(F32).rearrange("p (h n b u) -> p h n b u", h=2, n=2, u=2)
             for h in range(2):
-                xt = psum_x.tile([P, 2, 2, P], F32, name="xt")
-                for n in range(2):
-                    for u in range(2):
-                        nc.tensor.transpose(xt[:, n, u, :], words[:, GR * half + 2 * h + n, u, :], ident[:])
-                nc.vector.tensor_copy(out=dst[:, h], in_=xt[:].rearrange("p n u b -> p n b u"))
+                nc.vector.tensor_copy(out=dst[:, h], in_=x_bank[(q, h)][:].rearrange("p n u b -> p n b u"))
 
         def x_quant(q):
             x_codes[q] = xq_pool.tile([P, GR * P], U32, name="x_codes", align_bytes=64)
             x_scales[q] = xq_pool.tile([P, GR * P], U8, name="x_scales", align_bytes=64)
             nc.vector.quantize_mx(out=x_codes[q][:].bitcast(FP8X4), scales=x_scales[q][:], in_=x_grp[q][:])
 
-        def w_quant(q):
-            c, half = divmod(q, 2)
+        def w_quant(q, parts):
             w_codes[q] = wq_pool.tile([P, GR * COLS], U32, name="w_codes", align_bytes=64)
             w_scales[q] = wq_pool.tile([P, GR * COLS], U8, name="w_scales", align_bytes=64)
-            nc.vector.quantize_mx(
-                out=w_codes[q][:].bitcast(FP8X4),
-                scales=w_scales[q][:],
-                in_=w_grp[c][:, GR * half : GR * (half + 1)].rearrange("p n j c t -> p (n j c t)"),
+            caps = GR // parts
+            for k in range(parts):
+                cols = slice(k * caps * COLS, (k + 1) * caps * COLS)
+                nc.vector.quantize_mx(
+                    out=w_codes[q][:, cols].bitcast(FP8X4),
+                    scales=w_scales[q][:, cols],
+                    in_=w_grp[q][:, k * caps : (k + 1) * caps].rearrange("p n g c t -> p (n g c t)"),
+                )
+
+        def multiply(q, h, pool, tag):
+            bank = pool.tile([P, 2, COLS], F32, name=tag)
+            acc[(q, h)] = bank
+            for n in range(2):
+                a = 2 * h + n
+                nc.tensor.matmul_mx(
+                    out=bank[:, n, :],
+                    lhsT=x_codes[q][:, a * P : (a + 1) * P].bitcast(FP8X4),
+                    lhsT_scale=x_scales[q][:, a * P : (a + 1) * P],
+                    rhs=w_codes[q][:, a * COLS : (a + 1) * COLS].bitcast(FP8X4),
+                    rhs_scale=w_scales[q][:, a * COLS : (a + 1) * COLS],
+                    start=True,
+                    stop=True,
+                )
+
+        def evacuate(q, h, engine):
+            if q // 2 not in o_sb:
+                o_sb[q // 2] = o_pool.tile([P, 2 * GR, COLS], F32, name="o_sb")
+            res = o_sb[q // 2]
+            n0 = GR * (q % 2) + 2 * h
+            bank = acc[(q, h)]
+            if engine == "s":
+                for n in range(2):
+                    nc.scalar.copy(
+                        out=res[:, n0 + n, :].rearrange("p (m j e) -> p m j e", m=N_OUT, j=8),
+                        in_=bank[:, n, :].rearrange("p (j m e) -> p m j e", j=8, m=N_OUT),
+                    )
+            else:
+                nc.vector.tensor_copy(
+                    out=res[:, n0 : n0 + 2, :].rearrange("p n (m j e) -> p n m j e", m=N_OUT, j=8),
+                    in_=bank[:].rearrange("p n (j m e) -> p n m j e", j=8, m=N_OUT),
+                )
+
+        def store(n0, caps):
+            res = o_sb[n0 // (2 * GR)]
+            k0 = n0 % (2 * GR)
+            nc.sync.dma_start(
+                out=o_view[:, n0 * COLS : (n0 + caps) * COLS],
+                in_=res[:, k0 : k0 + caps, :].rearrange("p n c -> p (n c)"),
             )
 
-        def multiply(q):
-            c, half = divmod(q, 2)
-            last = c == N_CH - 1
-            if half == 0:
-                o_sb[c] = o_pool.tile([P, CH, COLS], F32, name="o_sb")
-            for h in range(2):
-                acc = psum_o.tile([P, 2, COLS], F32, name="acc")
-                for n in range(2):
-                    a = 2 * h + n
-                    nc.tensor.matmul_mx(
-                        out=acc[:, n, :],
-                        lhsT=x_codes[q][:, a * P : (a + 1) * P].bitcast(FP8X4),
-                        lhsT_scale=x_scales[q][:, a * P : (a + 1) * P],
-                        rhs=w_codes[q][:, a * COLS : (a + 1) * COLS].bitcast(FP8X4),
-                        rhs_scale=w_scales[q][:, a * COLS : (a + 1) * COLS],
-                        start=True,
-                        stop=True,
-                    )
-                n0 = GR * half + 2 * h
-                if last and h == 1:
-                    for n in range(2):
-                        nc.scalar.copy(
-                            out=o_sb[c][:, n0 + n, :].rearrange("p (m j e) -> p m j e", m=N_OUT, j=PAIRS),
-                            in_=acc[:, n, :].rearrange("p (j m e) -> p m j e", j=PAIRS, m=N_OUT),
-                        )
-                else:
-                    nc.vector.tensor_copy(
-                        out=o_sb[c][:, n0 : n0 + 2, :].rearrange("p n (m j e) -> p n m j e", m=N_OUT, j=PAIRS),
-                        in_=acc[:].rearrange("p n (j m e) -> p n m j e", j=PAIRS, m=N_OUT),
-                    )
-            if last:
-                nc.sync.dma_start(
-                    out=o_view[q], in_=o_sb[c][:, GR * half : GR * (half + 1), :].rearrange("p n c -> p (n c)")
-                )
-            elif half == 1:
-                nc.sync.dma_start(out=oc_view[c], in_=o_sb[c][:].rearrange("p n c -> p (n c)"))
+        x_units = [(0, 1), (1, 1)] + [(q, 2) for q in range(2, N_Q, 2)]
+        first_loads = []
+        for k in range(W_BUFS):
+            first_loads.append(("w", k))
+            for j in range(X_BUFS):
+                if x_units[j][0] == k:
+                    first_loads.append(("x", j))
 
         with tc.manual_schedule():
-            for c in range(W_BUFS):
-                load_w(c)
-                load_x(c)
-            for g in range(4):
-                w_bank(g)
-            for s in range(N_GR + 3):
-                if s < N_GR:
-                    x_group(s)
-                    if s % 2 == 1 and s // 2 + X_BUFS < N_CH:
-                        load_x(s // 2 + X_BUFS)
-                if 0 <= s - 2 < N_GR:
-                    w_quant(s - 2)
-                if s < N_GR:
-                    x_quant(s)
-                if 0 <= s - 3 < N_GR:
-                    multiply(s - 3)
-                if s < N_GR - 1:
-                    for g in range(4 * s + 4, 4 * s + 8):
-                        w_bank(g)
-                    if s % 2 == 0 and s // 2 + W_BUFS < N_CH:
-                        load_w(s // 2 + W_BUFS)
+            for kind, k in first_loads:
+                if kind == "w":
+                    load_w(k)
+                else:
+                    load_x(x_units[k][0], x_units[k][1])
+            w_transposes(0)
+            load_w(W_BUFS)
+            for s in range(N_Q):
+                last = s == N_Q - 1
+                x_transposes(s)
+                for k in range(X_BUFS, len(x_units)):
+                    freed = x_units[k - X_BUFS]
+                    if freed[0] + freed[1] - 1 == s:
+                        load_x(x_units[k][0], x_units[k][1])
+                for g in range(4):
+                    if ROUTE[s][g] != "s":
+                        w_copy(s, g)
+                x_copy(s)
+                if s >= 2:
+                    for h in range(2):
+                        multiply(s - 2, h, psum_o, "acc")
+                    for h in range(2):
+                        if EVAC[s - 2][h] == "v":
+                            evacuate(s - 2, h, "v")
+                for g in range(4):
+                    if ROUTE[s][g] == "s":
+                        w_copy(s, g)
+                if s >= 2:
+                    for h in range(2):
+                        if EVAC[s - 2][h] == "s":
+                            evacuate(s - 2, h, "s")
+                    if s % 2 == 1:
+                        store((s - 3) * GR, 2 * GR)
+                if s >= 1:
+                    w_quant(s - 1, 1)
+                x_quant(s)
+                if not last:
+                    w_transposes(s + 1)
+                    if s + 1 + W_BUFS < N_Q:
+                        load_w(s + 1 + W_BUFS)
+            q = N_Q - 2
+            multiply(q, 0, psum_o, "acc")
+            multiply(q, 1, psum_o, "acc")
+            w_quant(q + 1, 2)
+            evacuate(q, 0, "s")
+            evacuate(q, 1, "v")
+            store(q * GR, GR)
+            q = N_Q - 1
+            multiply(q, 0, psum_w, "wt")
+            multiply(q, 1, psum_w, "wt")
+            evacuate(q, 0, "s")
+            store(q * GR, 2)
+            evacuate(q, 1, "v")
+            store(q * GR + 2, 2)

@@ -21,8 +21,8 @@ GR = 4
 N_Q = N_IN // GR
 W_BUFS = 8
 X_BUFS = 5
-ROUTE = ["vsss","gsss","gsss","gsss","gsss","gsss","gsss","gsss","gsss","gsss","gsss","gsss","gsss","gsss","gsss","vsss"]
-EVAC = ["vs","vs","vs","vs","vs","vs","vs","vs","vs","vs","vs","vs","vs","ss","vs","vs"]
+ROUTE = ["vsss","vsss","vsss","vsss","vsss","vsss","vsss","vsss","vsss","vsss","vsss","vsss","vsss","vsss","vsss","vsss"]
+EVAC = ["ss","vs","ss","vs","ss","vs","ss","vs","ss","vs","ss","vs","ss","ss","ss","vs"]
 
 FLOPS = 2 * P * N_IN * D_IN * COLS
 

@@ -21,8 +21,8 @@ GR = 4
 N_Q = N_IN // GR
 W_BUFS = 8
 X_BUFS = 5
-ROUTE = ["vsss","vsss","vsss","vsss","vsss","vsss","vsss","vsss","vsss","vsss","vsss","vsss","vsss","vsss","vsss","vsss"]
-EVAC = ["ss","vs","ss","vs","ss","vs","ss","vs","ss","vs","ss","vs","ss","ss","ss","vs"]
+ROUTE = ["vsvs","gsss","gsss","gsss","gsss","gsss","gsss","gsss","gsss","gsss","gsss","gsss","gsss","gsss","gsss","vsss"]
+EVAC = ["vs","vs","ss","vs","vs","ss","vs","vs","ss","vs","vs","ss","vs","ss","vs","vs"]
 
 FLOPS = 2 * P * N_IN * D_IN * COLS
 

@@ -203,6 +203,9 @@ def tile_transforming_kernel(tc, inputs, transform_mat, out):
             load_w(W_BUFS)
             for s in range(N_Q):
                 last = s == N_Q - 1
+                if s >= 2:
+                    for h in range(2):
+                        multiply(s - 2, h, psum_o, "acc")
                 x_transposes(s)
                 for k in range(X_BUFS, len(x_units)):
                     freed = x_units[k - X_BUFS]
@@ -211,13 +214,11 @@ def tile_transforming_kernel(tc, inputs, transform_mat, out):
                 for g in range(4):
                     if ROUTE[s][g] != "s":
                         w_copy(s, g)
-                x_copy(s)
                 if s >= 2:
-                    for h in range(2):
-                        multiply(s - 2, h, psum_o, "acc")
                     for h in range(2):
                         if EVAC[s - 2][h] == "v":
                             evacuate(s - 2, h, "v")
+                x_copy(s)
                 for g in range(4):
                     if ROUTE[s][g] == "s":
                         w_copy(s, g)

from contextlib import ExitStack

import concourse.mybir as mybir
from concourse.masks import make_identity

F32 = mybir.dt.float32
BF16 = mybir.dt.bfloat16
U32 = mybir.dt.uint32
U8 = mybir.dt.uint8
FP8X4 = mybir.dt.float8_e4m3fn_x4
MULT = mybir.AluOpType.mult
ADD = mybir.AluOpType.add

P = 128
N_IN = 64
N_OUT = 16
D_IN = 512
D_OUT = 16
COLS = N_OUT * D_OUT
GR = 4
N_Q = N_IN // GR
W_BUFS = 8
X_BUFS = 5
ROUTE = ["vsvs","gsss","gsss","gsss","gsss","gsss","gsss","gsss","gsss","gsss","gsss","gsss","gsss","gsss","gsss","vsss"]
EVAC = ["vs","vs","ss","vs","vs","ss","vs","vs","ss","vs","vs","ss","vs","ss","vs","vs"]

FLOPS = 2 * P * N_IN * D_IN * COLS


def tile_transforming_kernel(tc, inputs, transform_mat, out):
    nc = tc.nc
    w_view = transform_mat.rearrange("z (q n) m (u i) o x -> q (z n m u) (i o x)", q=N_Q, u=2)
    x_view = inputs.rearrange("b n i x -> b (n i x)")
    o_view = out.rearrange("b n m o x -> b (n m o x)")

    with ExitStack() as stack:
        const = stack.enter_context(tc.tile_pool(name="const", bufs=1))
        w_pool = stack.enter_context(tc.tile_pool(name="w_pool", bufs=W_BUFS))
        x_pool = stack.enter_context(tc.tile_pool(name="x_pool", bufs=X_BUFS))
        g_pool = stack.enter_context(tc.tile_pool(name="g_pool", bufs=3))
        t_pool = stack.enter_context(tc.tile_pool(name="t_pool", bufs=2))
        xg_pool = stack.enter_context(tc.tile_pool(name="xg_pool", bufs=2))
        wq_pool = stack.enter_context(tc.tile_pool(name="wq_pool", bufs=3))
        xq_pool = stack.enter_context(tc.tile_pool(name="xq_pool", bufs=4))
        o_pool = stack.enter_context(tc.tile_pool(name="o_pool", bufs=5))
        psum_w = stack.enter_context(tc.psum_pool(name="psum_w", bufs=4))
        psum_x = stack.enter_context(tc.psum_pool(name="psum_x", bufs=2))
        psum_o = stack.enter_context(tc.psum_pool(name="psum_o", bufs=2))

        ident = const.tile([P, P], F32)
        make_identity(nc, ident[:])
        perm = const.tile([P, P], F32)
        nc.vector.tensor_copy(
            out=perm[:].rearrange("k (u g) -> k u g", u=2), in_=ident[:].rearrange("k (g u) -> k u g", u=2)
        )

        w_raw = {}
        x_raw = {}
        w_bank = {}
        x_bank = {}
        w_grp = {}
        w_codes = {}
        w_scales = {}
        x_codes = {}
        x_scales = {}
        x_grp = {}
        acc = {}
        o_sb = {}

        def load_w(q):
            w_raw[q] = w_pool.tile([P, D_IN * D_OUT // 2], BF16, name="w_raw")
            nc.sync.dma_start(out=w_raw[q][:], in_=w_view[q])

        def load_x(q0, nq):
            t = x_pool.tile([P, 2 * GR * D_IN], BF16, name="x_raw")
            width = nq * GR * D_IN
            nc.sync.dma_start(out=t[:, 0:width], in_=x_view[:, q0 * GR * D_IN : q0 * GR * D_IN + width])
            for k in range(nq):
                x_raw[q0 + k] = t[:, k * GR * D_IN : (k + 1) * GR * D_IN]

        def w_transposes(q):
            words = w_raw[q][:].bitcast(F32).rearrange("r (a e j) -> r e j a", e=2, j=8)
            for g in range(4):
                wt = psum_w.tile([P, 512], F32, name="wt")
                w_bank[(q, g)] = wt
                dst = wt[:].rearrange("p (u e n k m) -> p e k u n m", u=2, e=2, n=GR, k=2)
                for k in range(2):
                    for e in range(2):
                        nc.tensor.transpose(dst[:, e, k], words[:, e, 2 * g + k, :], perm[:])

        def w_copy(q, g):
            if q not in w_grp:
                w_grp[q] = g_pool.tile([P, GR, 4, 64, 4], BF16, name="w_grp", align_bytes=64)
            wt = w_bank[(q, g)]
            dst = w_grp[q][:, :, g, :, :]
            route = ROUTE[q][g]
            if route == "g":
                tmp = t_pool.tile([P, 512], F32, name="tmp")
                nc.vector.tensor_copy(out=tmp[:], in_=wt[:])
                nc.gpsimd.tensor_scalar(
                    out=dst,
                    in0=tmp[:].bitcast(BF16).rearrange("p (t n c) -> p n c t", t=4, n=GR),
                    scalar1=1.0,
                    scalar2=0.0,
                    op0=MULT,
                    op1=ADD,
                )
            else:
                src = wt[:].bitcast(BF16).rearrange("p (t n c) -> p n c t", t=4, n=GR)
                if route == "v":
                    nc.vector.tensor_copy(out=dst, in_=src)
                else:
                    nc.scalar.copy(out=dst, in_=src)

        def x_transposes(q):
            words = x_raw[q].bitcast(F32).rearrange("b (n u a) -> b n u a", n=GR, u=2)
            for h in range(2):
                xt = psum_x.tile([P, 2, 2, P], F32, name="xt")
                x_bank[(q, h)] = xt
                for n in range(2):
                    for u in range(2):
                        nc.tensor.transpose(xt[:, n, u, :], words[:, 2 * h + n, u, :], ident[:])

        def x_copy(q):
            x_grp[q] = xg_pool.tile([P, GR * D_IN], BF16, name="x_grp", align_bytes=64)
            dst = x_grp[q][:].bitcast(F32).rearrange("p (h n b u) -> p h n b u", h=2, n=2, u=2)
            for h in range(2):
                nc.vector.tensor_copy(out=dst[:, h], in_=x_bank[(q, h)][:].rearrange("p n u b -> p n b u"))

        def x_quant(q):
            x_codes[q] = xq_pool.tile([P, GR * P], U32, name="x_codes", align_bytes=64)
            x_scales[q] = xq_pool.tile([P, GR * P], U8, name="x_scales", align_bytes=64)
            nc.vector.quantize_mx(out=x_codes[q][:].bitcast(FP8X4), scales=x_scales[q][:], in_=x_grp[q][:])

        def w_quant(q, parts):
            w_codes[q] = wq_pool.tile([P, GR * COLS], U32, name="w_codes", align_bytes=64)
            w_scales[q] = wq_pool.tile([P, GR * COLS], U8, name="w_scales", align_bytes=64)
            caps = GR // parts
            for k in range(parts):
                cols = slice(k * caps * COLS, (k + 1) * caps * COLS)
                nc.vector.quantize_mx(
                    out=w_codes[q][:, cols].bitcast(FP8X4),
                    scales=w_scales[q][:, cols],
                    in_=w_grp[q][:, k * caps : (k + 1) * caps].rearrange("p n g c t -> p (n g c t)"),
                )

        def multiply(q, h, pool, tag):
            bank = pool.tile([P, 2, COLS], F32, name=tag)
            acc[(q, h)] = bank
            for n in range(2):
                a = 2 * h + n
                nc.tensor.matmul_mx(
                    out=bank[:, n, :],
                    lhsT=x_codes[q][:, a * P : (a + 1) * P].bitcast(FP8X4),
                    lhsT_scale=x_scales[q][:, a * P : (a + 1) * P],
                    rhs=w_codes[q][:, a * COLS : (a + 1) * COLS].bitcast(FP8X4),
                    rhs_scale=w_scales[q][:, a * COLS : (a + 1) * COLS],
                    start=True,
                    stop=True,
                )

        def evacuate(q, h, engine):
            if q // 2 not in o_sb:
                o_sb[q // 2] = o_pool.tile([P, 2 * GR, COLS], F32, name="o_sb")
            res = o_sb[q // 2]
            n0 = GR * (q % 2) + 2 * h
            bank = acc[(q, h)]
            if engine == "s":
                for n in range(2):
                    nc.scalar.copy(
                        out=res[:, n0 + n, :].rearrange("p (m j e) -> p m j e", m=N_OUT, j=8),
                        in_=bank[:, n, :].rearrange("p (j m e) -> p m j e", j=8, m=N_OUT),
                    )
            else:
                nc.vector.tensor_copy(
                    out=res[:, n0 : n0 + 2, :].rearrange("p n (m j e) -> p n m j e", m=N_OUT, j=8),
                    in_=bank[:].rearrange("p n (j m e) -> p n m j e", j=8, m=N_OUT),
                )

        def store(n0, caps):
            res = o_sb[n0 // (2 * GR)]
            k0 = n0 % (2 * GR)
            nc.sync.dma_start(
                out=o_view[:, n0 * COLS : (n0 + caps) * COLS],
                in_=res[:, k0 : k0 + caps, :].rearrange("p n c -> p (n c)"),
            )

        x_units = [(0, 1), (1, 1)] + [(q, 2) for q in range(2, N_Q, 2)]
        first_loads = []
        for k in range(W_BUFS):
            first_loads.append(("w", k))
            for j in range(X_BUFS):
                if x_units[j][0] == k:
                    first_loads.append(("x", j))

        with tc.manual_schedule():
            for kind, k in first_loads:
                if kind == "w":
                    load_w(k)
                else:
                    load_x(x_units[k][0], x_units[k][1])
            w_transposes(0)
            load_w(W_BUFS)
            for s in range(N_Q):
                last = s == N_Q - 1
                if s >= 2:
                    for h in range(2):
                        multiply(s - 2, h, psum_o, "acc")
                x_transposes(s)
                for k in range(X_BUFS, len(x_units)):
                    freed = x_units[k - X_BUFS]
                    if freed[0] + freed[1] - 1 == s:
                        load_x(x_units[k][0], x_units[k][1])
                for g in range(4):
                    if ROUTE[s][g] != "s":
                        w_copy(s, g)
                if s >= 2:
                    for h in range(2):
                        if EVAC[s - 2][h] == "v":
                            evacuate(s - 2, h, "v")
                x_copy(s)
                for g in range(4):
                    if ROUTE[s][g] == "s":
                        w_copy(s, g)
                if s >= 2:
                    for h in range(2):
                        if EVAC[s - 2][h] == "s":
                            evacuate(s - 2, h, "s")
                    if s % 2 == 1:
                        store((s - 3) * GR, 2 * GR)
                if s >= 1:
                    w_quant(s - 1, 1)
                x_quant(s)
                if not last:
                    w_transposes(s + 1)
                    if s + 1 + W_BUFS < N_Q:
                        load_w(s + 1 + W_BUFS)
            q = N_Q - 2
            multiply(q, 0, psum_o, "acc")
            multiply(q, 1, psum_o, "acc")
            w_quant(q + 1, 2)
            evacuate(q, 0, "s")
            evacuate(q, 1, "v")
            store(q * GR, GR)
            q = N_Q - 1
            multiply(q, 0, psum_w, "wt")
            multiply(q, 1, psum_w, "wt")
            evacuate(q, 0, "s")
            store(q * GR, 2)
            evacuate(q, 1, "v")
            store(q * GR + 2, 2)
